import numpy as np
import ml_dtypes


def mxq(x, axis, fmt="e4m3"):
    dtype, down = {"e4m3": (ml_dtypes.float8_e4m3fn, 7), "e5m2": (ml_dtypes.float8_e5m2, 14)}[fmt]
    v = np.moveaxis(np.asarray(x, np.float32).astype(ml_dtypes.bfloat16).astype(np.float64), axis, -1)
    blocks = v.reshape(v.shape[:-1] + (-1, 32))
    amax = np.abs(blocks).max(-1, keepdims=True)
    byte = np.maximum(np.where(amax > 0, np.frexp(amax)[1] - 1 + 127, 0) - down, 1)
    scale = np.exp2(byte - 127.0)
    codes = (blocks / scale).astype(np.float32).astype(dtype).astype(np.float64)
    return np.moveaxis((codes * scale).reshape(v.shape), -1, axis)


WIDE = False


def mx_kscale(k):
    if not WIDE:
        return np.ones(k)
    levels = np.array([18, -18])
    if k % 512:
        return np.exp2(np.random.permutation(np.resize(levels, k // 32))).repeat(32)
    a = np.empty((k // 512, 16))
    for p in range(k // 512):
        a[p, :8] = np.random.permutation(np.resize(levels, 8))
        for g in range(8):
            far = levels[np.abs(levels - a[p, g]) >= 10]
            a[p, g + 8] = far[np.random.randint(len(far))]
    return np.exp2(a.ravel()).repeat(32)


BF16 = ml_dtypes.bfloat16


def bf(x):
    return np.asarray(x, np.float32).astype(BF16)


def f64(x):
    return np.asarray(x).astype(np.float64)


B, C, H, W, S = 2, 512, 64, 32, 2
NB = (H // S) * (W // S)
T = B * NB


def spread(t):
    return np.repeat(np.repeat(t, S, axis=2), S, axis=3)


def block_mean(x):
    m = f64(x).reshape(B, C, H // S, S, W // S, S).mean(axis=(3, 5))
    return m.reshape(B, C, NB).transpose(0, 2, 1)


def setup_inputs():
    s = mx_kscale(T)
    u0 = mx_kscale(C)
    u1 = mx_kscale(C)
    st = s.reshape(B, NB, 1)
    sx = spread(s.reshape(B, 1, H // S, W // S))
    x = bf(np.random.standard_normal((B, C, H, W)) * sx)
    Wq = bf(np.random.standard_normal((C, C)) * 1.2 * S / np.sqrt(C) / u0[:, None])
    bq = bf(np.random.standard_normal(C) * 0.3)
    Wk = bf(np.random.standard_normal((C, C)) * 1.2 * S / np.sqrt(C) / u1[:, None])
    bk = bf(np.random.standard_normal(C) * 0.3)
    g0 = bf(np.random.standard_normal((B, NB, C)) * np.exp2(np.random.randint(-6, 1, (B, NB, 1))) / st * u0)
    g1 = bf(np.random.standard_normal((B, NB, C)) * np.exp2(np.random.randint(-6, 1, (B, NB, 1))) / st * u1)
    return {"x": x, "Wq": Wq, "bq": bq, "Wk": Wk, "bk": bk, "grad_0": g0, "grad_1": g1}


def reference(x, Wq, bq, Wk, bk, grad_0, grad_1):
    xq = mxq(block_mean(x).reshape(T, C), 0, "e4m3")
    g = np.concatenate([f64(grad_0).reshape(T, C), f64(grad_1).reshape(T, C)], axis=1)
    w = np.concatenate([f64(Wq), f64(Wk)], axis=0)
    da = mxq(g, 1, "e5m2") @ mxq(w, 0, "e4m3")
    dw = mxq(g, 0, "e5m2").T @ xq
    dx = spread(da.reshape(B, H // S, W // S, C).transpose(0, 3, 1, 2)) / (S * S)
    return dx, dw[:C], dw[C:]

@@ -1,0 +1,274 @@
+from contextlib import ExitStack
+
+import concourse.mybir as mybir
+from concourse.masks import make_identity
+
+B, C, H, W = 2, 512, 64, 32
+NB = (H // 2) * (W // 2)
+FLOPS = 2 * 2 * (B * NB) * (2 * C) * C
+BYTES = 2 * (B * C * H * W + 2 * C * C + 2 * B * NB * C) + 4 * (B * C * H * W + 2 * C * C)
+
+F32 = mybir.dt.float32
+BF16 = mybir.dt.bfloat16
+U32 = mybir.dt.uint32
+U8 = mybir.dt.uint8
+E4M3 = mybir.dt.float8_e4m3fn_x4
+E5M2 = mybir.dt.float8_e5m2_x4
+COPY = mybir.ActivationFunctionType.Copy
+ADD = mybir.AluOpType.add
+MULT = mybir.AluOpType.mult
+
+P = 128
+PACK = 4
+K_PASS = P * PACK
+QUARTER = 0.25
+
+
+def tile_coarseblockattention_pa_v_kernel(tc, x, Wq, bq, Wk, bk, grad_0, grad_1, out_0, out_1, out_2):
+    nc = tc.nc
+    weights = (Wq, Wk)
+    grads = (grad_0, grad_1)
+    dw_outs = (out_1, out_2)
+
+    with ExitStack() as ctx:
+        sb = ctx.enter_context(tc.tile_pool(name="sb", bufs=1))
+        ps = ctx.enter_context(tc.psum_pool(name="ps", bufs=1))
+        ctx.enter_context(tc.manual_schedule())
+
+        ident = sb.tile([P, P], F32, name="ident")
+        make_identity(nc, ident[:])
+
+        w_raw, g_raw, x_raw = {}, {}, {}
+        staged, mx = {}, {}
+        row_sums, pool_banks, da_bank, dx_tile = {}, {}, {}, {}
+        turn = {"transpose": 0}
+
+        def bank(n):
+            return ps.tile([P, 512], F32, name="bank%d" % n, tag="bank%d" % n)
+
+        def transpose_bank():
+            n = turn["transpose"]
+            turn.update({"transpose": n + 1})
+            return bank(n % 4)
+
+        def load_w(g):
+            t = sb.tile([P, PACK * C], BF16, name="w_raw%d" % g, align_bytes=256)
+            nc.sync.dma_start(out=t[:], in_=weights[g].rearrange("(p j) c -> p (j c)", j=PACK))
+            w_raw[g] = t
+
+        def load_g(g, b):
+            t = sb.tile([P, PACK * C], BF16, name="g_raw%d%d" % (g, b), align_bytes=256)
+            nc.sync.dma_start(out=t[:], in_=grads[g][b].rearrange("(p j) o -> p (j o)", j=PACK))
+            g_raw[(g, b)] = t
+
+        def load_x(b, half):
+            t = sb.tile([P, 2 * H * W], BF16, name="x_raw%d%d" % (b, half), align_bytes=256)
+            rows = x[b].rearrange("(p m) h w -> p (m h w)", m=4)
+            nc.sync.dma_start(out=t[:], in_=rows[:, half * 2 * H * W : (half + 1) * 2 * H * W])
+            x_raw[(b, half)] = t
+
+        def interleave(key, raw, shared=False):
+            t = sb.tile([P, PACK * C], BF16, name="interleaved", tag="interleaved", bufs=4, align_bytes=256)
+            dst = t[:].rearrange("p (c i t) -> p c t i", i=4, t=PACK)
+            src = raw[:].rearrange("p (t c i) -> p c t i", i=4, t=PACK)
+            if shared:
+                nc.vector.tensor_copy(out=dst[:, :64], in_=src[:, :64])
+                nc.scalar.copy(out=dst[:, 64:], in_=src[:, 64:])
+            else:
+                nc.vector.tensor_copy(out=dst, in_=src)
+            staged[key] = t
+
+        def quantize(key, fmt):
+            name = "_".join(str(k) for k in key)
+            codes = sb.tile([P, 512], U32, name="codes_" + name, align_bytes=256)
+            scales = sb.tile([P, 512], U8, name="scales_" + name, align_bytes=256)
+            nc.vector.quantize_mx(out=codes[:].bitcast(fmt), scales=scales[:], in_=staged[key][:])
+            mx[key] = (codes, scales, fmt)
+
+        def transpose_g(g, b):
+            t = sb.tile([P, PACK * NB], BF16, name="g_feat%d%d" % (g, b), align_bytes=256)
+            words = g_raw[(g, b)][:].bitcast(F32)
+            dst = t[:].bitcast(F32).rearrange("q (p j u) -> q p j u", j=PACK, u=2)
+            for pair in range(2):
+                bk_t = transpose_bank()
+                for jj in range(2):
+                    for u in range(2):
+                        j = 2 * pair + jj
+                        s = 2 * jj + u
+                        nc.tensor.transpose(
+                            bk_t[:, s * P : (s + 1) * P], words[:, 256 * j + u : 256 * (j + 1) : 2], ident[:]
+                        )
+                nc.scalar.copy(
+                    out=dst[:, :, 2 * pair : 2 * pair + 2, :],
+                    in_=bk_t[:].rearrange("q (j u p) -> q p j u", j=2, u=2),
+                )
+            staged[("gf", g, b)] = t
+
+        def mm(acc, lhs, cols, rhs, start, stop):
+            lc, ls, lf = mx[lhs]
+            rc, rs, rf = mx[rhs]
+            nc.tensor.matmul_mx(
+                out=acc[:],
+                lhsT=lc[:, cols].bitcast(lf),
+                lhsT_scale=ls[:, cols],
+                rhs=rc[:].bitcast(rf),
+                rhs_scale=rs[:],
+                start=start,
+                stop=stop,
+            )
+
+        def da_matmuls(b, m):
+            acc = bank(4 + m)
+            for g in range(2):
+                mm(acc, ("w", g), slice(m * P, (m + 1) * P), ("gf", g, b), g == 0, g == 1)
+            da_bank[(b, m)] = acc
+
+        def spread_row(b, m, i):
+            if i == 0:
+                dx_tile[(b, m)] = sb.tile([P, H * W], F32, name="dx%d%d" % (b, m), align_bytes=256)
+            view = dx_tile[(b, m)][:].rearrange("p (h i w j) -> p h i w j", i=2, w=W // 2, j=2)
+            src = da_bank[(b, m)][:].rearrange("p (h w) -> p h w", w=W // 2).unsqueeze(3).to_broadcast([P, H // 2, W // 2, 2])
+            nc.scalar.activation(out=view[:, :, i, :, :], in_=src, func=COPY, scale=QUARTER)
+
+        def repeat_row(b, m):
+            view = dx_tile[(b, m)][:].rearrange("p (h i w) -> p h i w", i=2, w=W)
+            nc.vector.tensor_copy(out=view[:, :, 1, :], in_=view[:, :, 0, :])
+
+        def store_dx(b, m):
+            nc.sync.dma_start(
+                out=out_0[b, m * P : (m + 1) * P].rearrange("c h w -> c (h w)"), in_=dx_tile[(b, m)][:]
+            )
+
+        def add_rows(b, half):
+            v = x_raw[(b, half)][:].rearrange("p (a i q t j) -> p a i q t j", i=2, q=4, t=PACK, j=2)
+            for t in range(PACK):
+                r = sb.tile([P, 512], F32, name="row_sum%d" % t, tag="row_sum%d" % t, bufs=2, align_bytes=256)
+                nc.vector.tensor_tensor(
+                    out=r[:].rearrange("p (a q j) -> p a q j", q=4, j=2),
+                    in0=v[:, :, 0, :, t, :],
+                    in1=v[:, :, 1, :, t, :],
+                    op=ADD,
+                )
+                row_sums[(b, half, t)] = r
+
+        def pool_transposes(b, half):
+            banks = [transpose_bank(), transpose_bank()]
+            for t in range(PACK):
+                r = row_sums[(b, half, t)]
+                for k in range(2):
+                    for j in range(2):
+                        nc.tensor.matmul(
+                            banks[k][:, t * P : (t + 1) * P],
+                            lhsT=r[:, 256 * k + j : 256 * (k + 1) : 2],
+                            rhs=ident[:],
+                            is_transpose=True,
+                            start=(j == 0),
+                            stop=(j == 1),
+                        )
+            pool_banks[(b, half)] = banks
+
+        def pool_means(b, half):
+            if half == 0:
+                staged[("a", b)] = sb.tile([P, PACK * C], BF16, name="a_mean%d" % b, align_bytes=256)
+            for k in range(2):
+                m = 2 * half + k
+                nc.scalar.activation(
+                    out=staged[("a", b)][:, m * 512 : (m + 1) * 512].rearrange("p (c t) -> p c t", t=PACK),
+                    in_=pool_banks[(b, half)][k][:].rearrange("p (t c) -> p c t", t=PACK),
+                    func=COPY,
+                    scale=QUARTER,
+                )
+
+        def dw_rows(g, half):
+            res = sb.tile([P, 2 * C], F32, name="dw%d%d" % (g, half), align_bytes=256)
+            for k in range(2):
+                mo = 2 * half + k
+                acc = bank(4 * g + mo)
+                for b in range(B):
+                    mm(acc, ("gt", g, b), slice(mo * P, (mo + 1) * P), ("a", b), b == 0, b == B - 1)
+                dst = res[:, k * C : (k + 1) * C].rearrange("p (c m) -> p c m", m=4)
+                src = acc[:].rearrange("p (m c) -> p c m", m=4)
+                if k == 0:
+                    nc.scalar.copy(out=dst, in_=src)
+                else:
+                    nc.vector.tensor_copy(out=dst, in_=src)
+            nc.sync.dma_start(
+                out=dw_outs[g][half * 2 * P : (half + 1) * 2 * P, :].rearrange("(k p) c -> p k c", p=P),
+                in_=res[:].rearrange("p (k c) -> p k c", k=2),
+            )
+
+        load_w(0)
+        load_g(0, 0)
+        load_w(1)
+        load_g(1, 0)
+        load_g(0, 1)
+        load_g(1, 1)
+        for b in range(B):
+            for half in range(2):
+                load_x(b, half)
+
+        def spread_both(b, m):
+            spread_row(b, m, 0)
+            spread_row(b, m, 1)
+            store_dx(b, m)
+
+        def finish(b, m):
+            repeat_row(b, m)
+            store_dx(b, m)
+
+        interleave(("w", 0), w_raw[0], shared=True)
+        interleave(("gt", 0, 0), g_raw[(0, 0)])
+        transpose_g(0, 0)
+        quantize(("w", 0), E4M3)
+        interleave(("w", 1), w_raw[1], shared=True)
+        transpose_g(1, 0)
+        quantize(("gf", 0, 0), E5M2)
+        quantize(("w", 1), E4M3)
+        quantize(("gt", 0, 0), E5M2)
+        quantize(("gf", 1, 0), E5M2)
+        transpose_g(0, 1)
+        transpose_g(1, 1)
+        for m in range(4):
+            da_matmuls(0, m)
+        interleave(("gt", 1, 0), g_raw[(1, 0)])
+        quantize(("gf", 0, 1), E5M2)
+        quantize(("gf", 1, 1), E5M2)
+
+        add_rows(0, 0)
+        quantize(("gt", 1, 0), E5M2)
+        spread_both(0, 0)
+        da_matmuls(1, 0)
+        pool_transposes(0, 0)
+        spread_both(0, 1)
+        da_matmuls(1, 1)
+        add_rows(0, 1)
+        pool_transposes(0, 1)
+        spread_both(0, 2)
+        da_matmuls(1, 2)
+        pool_means(0, 0)
+        add_rows(1, 0)
+        pool_transposes(1, 0)
+        spread_both(0, 3)
+        da_matmuls(1, 3)
+        spread_row(1, 0, 0)
+        pool_means(0, 1)
+        add_rows(1, 1)
+        pool_transposes(1, 1)
+        spread_row(1, 1, 0)
+        pool_means(1, 0)
+        spread_row(1, 2, 0)
+        pool_means(1, 1)
+        spread_row(1, 3, 0)
+        finish(1, 0)
+        interleave(("gt", 0, 1), g_raw[(0, 1)])
+        quantize(("a", 0), E4M3)
+        finish(1, 1)
+        interleave(("gt", 1, 1), g_raw[(1, 1)])
+        finish(1, 2)
+        quantize(("gt", 0, 1), E5M2)
+        quantize(("a", 1), E4M3)
+        quantize(("gt", 1, 1), E5M2)
+        finish(1, 3)
+        for g in range(2):
+            for half in range(2):
+                dw_rows(g, half)

@@ -22,6 +22,7 @@ P = 128
 PACK = 4
 K_PASS = P * PACK
 QUARTER = 0.25
+DW_BANKS = (4, 0, 1, 5, 2, 3, 6, 7)
 
 
 def tile_coarseblockattention_pa_v_kernel(tc, x, Wq, bq, Wk, bk, grad_0, grad_1, out_0, out_1, out_2):
@@ -40,7 +41,7 @@ def tile_coarseblockattention_pa_v_kernel(tc, x, Wq, bq, Wk, bk, grad_0, grad_1,
 
         w_raw, g_raw, x_raw = {}, {}, {}
         staged, mx = {}, {}
-        row_sums, pool_banks, da_bank, dx_tile = {}, {}, {}, {}
+        row_sums, pool_banks, da_bank, dw_bank, dx_tile = {}, {}, {}, {}, {}
         turn = {"transpose": 0}
 
         def bank(n):
@@ -61,11 +62,10 @@ def tile_coarseblockattention_pa_v_kernel(tc, x, Wq, bq, Wk, bk, grad_0, grad_1,
             nc.sync.dma_start(out=t[:], in_=grads[g][b].rearrange("(p j) o -> p (j o)", j=PACK))
             g_raw[(g, b)] = t
 
-        def load_x(b, half):
-            t = sb.tile([P, 2 * H * W], BF16, name="x_raw%d%d" % (b, half), align_bytes=256)
-            rows = x[b].rearrange("(p m) h w -> p (m h w)", m=4)
-            nc.sync.dma_start(out=t[:], in_=rows[:, half * 2 * H * W : (half + 1) * 2 * H * W])
-            x_raw[(b, half)] = t
+        def load_x(b):
+            t = sb.tile([P, 4 * H * W], BF16, name="x_raw%d" % b, align_bytes=256)
+            nc.sync.dma_start(out=t[:], in_=x[b].rearrange("(p m) h w -> p (m h w)", m=4))
+            x_raw[b] = t
 
         def interleave(key, raw, shared=False):
             t = sb.tile([P, PACK * C], BF16, name="interleaved", tag="interleaved", bufs=4, align_bytes=256)
@@ -140,11 +140,11 @@ def tile_coarseblockattention_pa_v_kernel(tc, x, Wq, bq, Wk, bk, grad_0, grad_1,
             )
 
         def add_rows(b, half):
-            v = x_raw[(b, half)][:].rearrange("p (a i q t j) -> p a i q t j", i=2, q=4, t=PACK, j=2)
+            v = x_raw[b][:, half * 2 * H * W : (half + 1) * 2 * H * W].rearrange("p (a i q t j) -> p a i q t j", i=2, q=4, t=PACK, j=2)
             for t in range(PACK):
                 r = sb.tile([P, 512], F32, name="row_sum%d" % t, tag="row_sum%d" % t, bufs=2, align_bytes=256)
                 nc.vector.tensor_tensor(
-                    out=r[:].rearrange("p (a q j) -> p a q j", q=4, j=2),
+                    out=r[:].rearrange("p (j a q) -> p a q j", q=4, j=2),
                     in0=v[:, :, 0, :, t, :],
                     in1=v[:, :, 1, :, t, :],
                     op=ADD,
@@ -159,7 +159,7 @@ def tile_coarseblockattention_pa_v_kernel(tc, x, Wq, bq, Wk, bk, grad_0, grad_1,
                     for j in range(2):
                         nc.tensor.matmul(
                             banks[k][:, t * P : (t + 1) * P],
-                            lhsT=r[:, 256 * k + j : 256 * (k + 1) : 2],
+                            lhsT=r[:, (2 * j + k) * P : (2 * j + k + 1) * P],
                             rhs=ident[:],
                             is_transpose=True,
                             start=(j == 0),
@@ -179,15 +179,17 @@ def tile_coarseblockattention_pa_v_kernel(tc, x, Wq, bq, Wk, bk, grad_0, grad_1,
                     scale=QUARTER,
                 )
 
+        def dw_pass(n, b):
+            g, mo = divmod(n, 4)
+            if b == 0:
+                dw_bank[n] = bank(DW_BANKS[n])
+            mm(dw_bank[n], ("gt", g, b), slice(mo * P, (mo + 1) * P), ("a", b), b == 0, b == B - 1)
+
         def dw_rows(g, half):
             res = sb.tile([P, 2 * C], F32, name="dw%d%d" % (g, half), align_bytes=256)
             for k in range(2):
-                mo = 2 * half + k
-                acc = bank(4 * g + mo)
-                for b in range(B):
-                    mm(acc, ("gt", g, b), slice(mo * P, (mo + 1) * P), ("a", b), b == 0, b == B - 1)
                 dst = res[:, k * C : (k + 1) * C].rearrange("p (c m) -> p c m", m=4)
-                src = acc[:].rearrange("p (m c) -> p c m", m=4)
+                src = dw_bank[4 * g + 2 * half + k][:].rearrange("p (m c) -> p c m", m=4)
                 if k == 0:
                     nc.scalar.copy(out=dst, in_=src)
                 else:
@@ -204,8 +206,7 @@ def tile_coarseblockattention_pa_v_kernel(tc, x, Wq, bq, Wk, bk, grad_0, grad_1,
         load_g(0, 1)
         load_g(1, 1)
         for b in range(B):
-            for half in range(2):
-                load_x(b, half)
+            load_x(b)
 
         def spread_both(b, m):
             spread_row(b, m, 0)
@@ -234,8 +235,9 @@ def tile_coarseblockattention_pa_v_kernel(tc, x, Wq, bq, Wk, bk, grad_0, grad_1,
         quantize(("gf", 0, 1), E5M2)
         quantize(("gf", 1, 1), E5M2)
 
-        add_rows(0, 0)
+        interleave(("gt", 0, 1), g_raw[(0, 1)])
         quantize(("gt", 1, 0), E5M2)
+        add_rows(0, 0)
         spread_both(0, 0)
         da_matmuls(1, 0)
         pool_transposes(0, 0)
@@ -252,6 +254,8 @@ def tile_coarseblockattention_pa_v_kernel(tc, x, Wq, bq, Wk, bk, grad_0, grad_1,
         da_matmuls(1, 3)
         spread_row(1, 0, 0)
         pool_means(0, 1)
+        interleave(("gt", 1, 1), g_raw[(1, 1)])
+        finish(1, 0)
         add_rows(1, 1)
         pool_transposes(1, 1)
         spread_row(1, 1, 0)
@@ -259,16 +263,21 @@ def tile_coarseblockattention_pa_v_kernel(tc, x, Wq, bq, Wk, bk, grad_0, grad_1,
         spread_row(1, 2, 0)
         pool_means(1, 1)
         spread_row(1, 3, 0)
-        finish(1, 0)
-        interleave(("gt", 0, 1), g_raw[(0, 1)])
-        quantize(("a", 0), E4M3)
         finish(1, 1)
-        interleave(("gt", 1, 1), g_raw[(1, 1)])
-        finish(1, 2)
+        quantize(("a", 0), E4M3)
         quantize(("gt", 0, 1), E5M2)
-        quantize(("a", 1), E4M3)
+        finish(1, 2)
         quantize(("gt", 1, 1), E5M2)
+        quantize(("a", 1), E4M3)
         finish(1, 3)
+        for n in range(6):
+            dw_pass(n, 0)
+        for n in range(4):
+            dw_pass(n, 1)
+        for n in range(6, 8):
+            dw_pass(n, 0)
+        for n in range(4, 8):
+            dw_pass(n, 1)
         for g in range(2):
             for half in range(2):
                 dw_rows(g, half)

from contextlib import ExitStack

import concourse.mybir as mybir
from concourse.masks import make_identity

B, C, H, W = 2, 512, 64, 32
NB = (H // 2) * (W // 2)
FLOPS = 2 * 2 * (B * NB) * (2 * C) * C
BYTES = 2 * (B * C * H * W + 2 * C * C + 2 * B * NB * C) + 4 * (B * C * H * W + 2 * C * C)

F32 = mybir.dt.float32
BF16 = mybir.dt.bfloat16
U32 = mybir.dt.uint32
U8 = mybir.dt.uint8
E4M3 = mybir.dt.float8_e4m3fn_x4
E5M2 = mybir.dt.float8_e5m2_x4
COPY = mybir.ActivationFunctionType.Copy
ADD = mybir.AluOpType.add
MULT = mybir.AluOpType.mult

P = 128
PACK = 4
K_PASS = P * PACK
QUARTER = 0.25
DW_BANKS = (4, 0, 1, 5, 2, 3, 6, 7)


def tile_coarseblockattention_pa_v_kernel(tc, x, Wq, bq, Wk, bk, grad_0, grad_1, out_0, out_1, out_2):
    nc = tc.nc
    weights = (Wq, Wk)
    grads = (grad_0, grad_1)
    dw_outs = (out_1, out_2)

    with ExitStack() as ctx:
        sb = ctx.enter_context(tc.tile_pool(name="sb", bufs=1))
        ps = ctx.enter_context(tc.psum_pool(name="ps", bufs=1))
        ctx.enter_context(tc.manual_schedule())

        ident = sb.tile([P, P], F32, name="ident")
        make_identity(nc, ident[:])

        w_raw, g_raw, x_raw = {}, {}, {}
        staged, mx = {}, {}
        row_sums, pool_banks, da_bank, dw_bank, dx_tile = {}, {}, {}, {}, {}
        turn = {"transpose": 0}

        def bank(n):
            return ps.tile([P, 512], F32, name="bank%d" % n, tag="bank%d" % n)

        def transpose_bank():
            n = turn["transpose"]
            turn.update({"transpose": n + 1})
            return bank(n % 4)

        def load_w(g):
            t = sb.tile([P, PACK * C], BF16, name="w_raw%d" % g, align_bytes=256)
            nc.sync.dma_start(out=t[:], in_=weights[g].rearrange("(p j) c -> p (j c)", j=PACK))
            w_raw[g] = t

        def load_g(g, b):
            t = sb.tile([P, PACK * C], BF16, name="g_raw%d%d" % (g, b), align_bytes=256)
            nc.sync.dma_start(out=t[:], in_=grads[g][b].rearrange("(p j) o -> p (j o)", j=PACK))
            g_raw[(g, b)] = t

        def load_x(b):
            t = sb.tile([P, 4 * H * W], BF16, name="x_raw%d" % b, align_bytes=256)
            nc.sync.dma_start(out=t[:], in_=x[b].rearrange("(p m) h w -> p (m h w)", m=4))
            x_raw[b] = t

        def interleave(key, raw, shared=False):
            t = sb.tile([P, PACK * C], BF16, name="interleaved", tag="interleaved", bufs=4, align_bytes=256)
            dst = t[:].rearrange("p (c i t) -> p c t i", i=4, t=PACK)
            src = raw[:].rearrange("p (t c i) -> p c t i", i=4, t=PACK)
            if shared:
                nc.vector.tensor_copy(out=dst[:, :64], in_=src[:, :64])
                nc.scalar.copy(out=dst[:, 64:], in_=src[:, 64:])
            else:
                nc.vector.tensor_copy(out=dst, in_=src)
            staged[key] = t

        def quantize(key, fmt):
            name = "_".join(str(k) for k in key)
            codes = sb.tile([P, 512], U32, name="codes_" + name, align_bytes=256)
            scales = sb.tile([P, 512], U8, name="scales_" + name, align_bytes=256)
            nc.vector.quantize_mx(out=codes[:].bitcast(fmt), scales=scales[:], in_=staged[key][:])
            mx[key] = (codes, scales, fmt)

        def transpose_g(g, b):
            t = sb.tile([P, PACK * NB], BF16, name="g_feat%d%d" % (g, b), align_bytes=256)
            words = g_raw[(g, b)][:].bitcast(F32)
            dst = t[:].bitcast(F32).rearrange("q (p j u) -> q p j u", j=PACK, u=2)
            for pair in range(2):
                bk_t = transpose_bank()
                for jj in range(2):
                    for u in range(2):
                        j = 2 * pair + jj
                        s = 2 * jj + u
                        nc.tensor.transpose(
                            bk_t[:, s * P : (s + 1) * P], words[:, 256 * j + u : 256 * (j + 1) : 2], ident[:]
                        )
                nc.scalar.copy(
                    out=dst[:, :, 2 * pair : 2 * pair + 2, :],
                    in_=bk_t[:].rearrange("q (j u p) -> q p j u", j=2, u=2),
                )
            staged[("gf", g, b)] = t

        def mm(acc, lhs, cols, rhs, start, stop):
            lc, ls, lf = mx[lhs]
            rc, rs, rf = mx[rhs]
            nc.tensor.matmul_mx(
                out=acc[:],
                lhsT=lc[:, cols].bitcast(lf),
                lhsT_scale=ls[:, cols],
                rhs=rc[:].bitcast(rf),
                rhs_scale=rs[:],
                start=start,
                stop=stop,
            )

        def da_matmuls(b, m):
            acc = bank(4 + m)
            for g in range(2):
                mm(acc, ("w", g), slice(m * P, (m + 1) * P), ("gf", g, b), g == 0, g == 1)
            da_bank[(b, m)] = acc

        def spread_row(b, m, i):
            if i == 0:
                dx_tile[(b, m)] = sb.tile([P, H * W], F32, name="dx%d%d" % (b, m), align_bytes=256)
            view = dx_tile[(b, m)][:].rearrange("p (h i w j) -> p h i w j", i=2, w=W // 2, j=2)
            src = da_bank[(b, m)][:].rearrange("p (h w) -> p h w", w=W // 2).unsqueeze(3).to_broadcast([P, H // 2, W // 2, 2])
            nc.scalar.activation(out=view[:, :, i, :, :], in_=src, func=COPY, scale=QUARTER)

        def repeat_row(b, m):
            view = dx_tile[(b, m)][:].rearrange("p (h i w) -> p h i w", i=2, w=W)
            nc.vector.tensor_copy(out=view[:, :, 1, :], in_=view[:, :, 0, :])

        def store_dx(b, m):
            nc.sync.dma_start(
                out=out_0[b, m * P : (m + 1) * P].rearrange("c h w -> c (h w)"), in_=dx_tile[(b, m)][:]
            )

        def add_rows(b, half):
            v = x_raw[b][:, half * 2 * H * W : (half + 1) * 2 * H * W].rearrange("p (a i q t j) -> p a i q t j", i=2, q=4, t=PACK, j=2)
            for t in range(PACK):
                r = sb.tile([P, 512], F32, name="row_sum%d" % t, tag="row_sum%d" % t, bufs=2, align_bytes=256)
                nc.vector.tensor_tensor(
                    out=r[:].rearrange("p (j a q) -> p a q j", q=4, j=2),
                    in0=v[:, :, 0, :, t, :],
                    in1=v[:, :, 1, :, t, :],
                    op=ADD,
                )
                row_sums[(b, half, t)] = r

        def pool_transposes(b, half):
            banks = [transpose_bank(), transpose_bank()]
            for t in range(PACK):
                r = row_sums[(b, half, t)]
                for k in range(2):
                    for j in range(2):
                        nc.tensor.matmul(
                            banks[k][:, t * P : (t + 1) * P],
                            lhsT=r[:, (2 * j + k) * P : (2 * j + k + 1) * P],
                            rhs=ident[:],
                            is_transpose=True,
                            start=(j == 0),
                            stop=(j == 1),
                        )
            pool_banks[(b, half)] = banks

        def pool_means(b, half):
            if half == 0:
                staged[("a", b)] = sb.tile([P, PACK * C], BF16, name="a_mean%d" % b, align_bytes=256)
            for k in range(2):
                m = 2 * half + k
                nc.scalar.activation(
                    out=staged[("a", b)][:, m * 512 : (m + 1) * 512].rearrange("p (c t) -> p c t", t=PACK),
                    in_=pool_banks[(b, half)][k][:].rearrange("p (t c) -> p c t", t=PACK),
                    func=COPY,
                    scale=QUARTER,
                )

        def dw_pass(n, b):
            g, mo = divmod(n, 4)
            if b == 0:
                dw_bank[n] = bank(DW_BANKS[n])
            mm(dw_bank[n], ("gt", g, b), slice(mo * P, (mo + 1) * P), ("a", b), b == 0, b == B - 1)

        def dw_rows(g, half):
            res = sb.tile([P, 2 * C], F32, name="dw%d%d" % (g, half), align_bytes=256)
            for k in range(2):
                dst = res[:, k * C : (k + 1) * C].rearrange("p (c m) -> p c m", m=4)
                src = dw_bank[4 * g + 2 * half + k][:].rearrange("p (m c) -> p c m", m=4)
                if k == 0:
                    nc.scalar.copy(out=dst, in_=src)
                else:
                    nc.vector.tensor_copy(out=dst, in_=src)
            nc.sync.dma_start(
                out=dw_outs[g][half * 2 * P : (half + 1) * 2 * P, :].rearrange("(k p) c -> p k c", p=P),
                in_=res[:].rearrange("p (k c) -> p k c", k=2),
            )

        load_w(0)
        load_g(0, 0)
        load_w(1)
        load_g(1, 0)
        load_g(0, 1)
        load_g(1, 1)
        for b in range(B):
            load_x(b)

        def spread_both(b, m):
            spread_row(b, m, 0)
            spread_row(b, m, 1)
            store_dx(b, m)

        def finish(b, m):
            repeat_row(b, m)
            store_dx(b, m)

        interleave(("w", 0), w_raw[0], shared=True)
        interleave(("gt", 0, 0), g_raw[(0, 0)])
        transpose_g(0, 0)
        quantize(("w", 0), E4M3)
        interleave(("w", 1), w_raw[1], shared=True)
        transpose_g(1, 0)
        quantize(("gf", 0, 0), E5M2)
        quantize(("w", 1), E4M3)
        quantize(("gt", 0, 0), E5M2)
        quantize(("gf", 1, 0), E5M2)
        transpose_g(0, 1)
        transpose_g(1, 1)
        for m in range(4):
            da_matmuls(0, m)
        interleave(("gt", 1, 0), g_raw[(1, 0)])
        quantize(("gf", 0, 1), E5M2)
        quantize(("gf", 1, 1), E5M2)

        interleave(("gt", 0, 1), g_raw[(0, 1)])
        quantize(("gt", 1, 0), E5M2)
        add_rows(0, 0)
        spread_both(0, 0)
        da_matmuls(1, 0)
        pool_transposes(0, 0)
        spread_both(0, 1)
        da_matmuls(1, 1)
        add_rows(0, 1)
        pool_transposes(0, 1)
        spread_both(0, 2)
        da_matmuls(1, 2)
        pool_means(0, 0)
        add_rows(1, 0)
        pool_transposes(1, 0)
        spread_both(0, 3)
        da_matmuls(1, 3)
        spread_row(1, 0, 0)
        pool_means(0, 1)
        interleave(("gt", 1, 1), g_raw[(1, 1)])
        finish(1, 0)
        add_rows(1, 1)
        pool_transposes(1, 1)
        spread_row(1, 1, 0)
        pool_means(1, 0)
        spread_row(1, 2, 0)
        pool_means(1, 1)
        spread_row(1, 3, 0)
        finish(1, 1)
        quantize(("a", 0), E4M3)
        quantize(("gt", 0, 1), E5M2)
        finish(1, 2)
        quantize(("gt", 1, 1), E5M2)
        quantize(("a", 1), E4M3)
        finish(1, 3)
        for n in range(6):
            dw_pass(n, 0)
        for n in range(4):
            dw_pass(n, 1)
        for n in range(6, 8):
            dw_pass(n, 0)
        for n in range(4, 8):
            dw_pass(n, 1)
        for g in range(2):
            for half in range(2):
                dw_rows(g, half)
